import numpy as np
import ml_dtypes

BF16 = ml_dtypes.bfloat16


def bf(x):
    return np.asarray(x, np.float32).astype(BF16)


def f32(x):
    return np.asarray(x, np.float32)


def f64(x):
    return np.asarray(x).astype(np.float64)


def striped(idx):
    return np.tile(idx.reshape(-1, 16).T, (8, 1))


D, S, M, N = 128, 256, 512, 512


def sigmoid(v):
    return 1.0 / (1.0 + np.exp(-v))


def setup_inputs():
    return {"w_parent": bf(np.random.standard_normal((D, S)) / np.sqrt(D)), "patients": bf(np.random.standard_normal((D, M))), "w_child": bf(np.random.standard_normal((D, N)) / np.sqrt(D)), "b_child": f32(0.1 * np.random.standard_normal((1, N))), "offs": striped(np.random.permutation(np.tile(np.arange(S), 2))[:N])}


def reference(w_parent, patients, w_child, b_child, offs):
    idx = offs[:16].T.reshape(-1)
    p = f64(patients)
    parent = sigmoid(p.T @ f64(w_parent)[:, idx])
    child = sigmoid(p.T @ f64(w_child) + f64(b_child))
    return child * parent

@@ -1,0 +1,69 @@
+import concourse.mybir as mybir
+
+BF16, F32, U16 = mybir.dt.bfloat16, mybir.dt.float32, mybir.dt.uint16
+SIGMOID = mybir.ActivationFunctionType.Sigmoid
+ADD, MULT = mybir.AluOpType.add, mybir.AluOpType.mult
+
+P = 128
+PARENTS = 256
+PATIENTS = 512
+CHILDREN = 512
+BLOCKS = PATIENTS // P
+PIECE = PARENTS
+PIECES = CHILDREN // PIECE
+PIECE_COLS = PIECE // 16
+
+FLOPS = 2 * P * PATIENTS * CHILDREN * 2
+
+
+def tile_hierarchicaldecoder_kernel(tc, w_parent, patients, w_child, b_child, offs, out):
+    nc = tc.nc
+    with (
+        tc.tile_pool(name="held", bufs=1) as held,
+        tc.tile_pool(name="work", bufs=BLOCKS) as work,
+        tc.psum_pool(name="psum", bufs=BLOCKS) as psum,
+    ):
+        offsets = held.tile([P, CHILDREN // 16], U16, name="offsets")
+        nc.sync.dma_start(offsets[:], offs)
+        patient_cols = held.tile([P, PATIENTS], BF16, name="patient_cols")
+        nc.scalar.dma_start(patient_cols[:], patients)
+        parent_table = held.tile([P, PARENTS], BF16, name="parent_table")
+        nc.sync.dma_start(parent_table[:], w_parent)
+        child_weights = held.tile([P, CHILDREN], BF16, name="child_weights")
+        nc.scalar.dma_start(child_weights[:], w_child)
+        bias_rows = held.tile([P, CHILDREN], F32, name="bias_rows")
+        nc.gpsimd.dma_start(bias_rows[:], b_child.broadcast_to([P, CHILDREN]))
+
+        parent_logits = []
+        for b in range(BLOCKS):
+            bank = psum.tile([P, CHILDREN], F32, name="parent_bank")
+            for piece in range(PIECES):
+                nc.tensor.matmul(
+                    bank[:, piece * PIECE : (piece + 1) * PIECE],
+                    patient_cols[:, b * P : (b + 1) * P],
+                    parent_table[:].indirect(offsets[:, piece * PIECE_COLS : (piece + 1) * PIECE_COLS]),
+                    start=True,
+                    stop=True,
+                )
+            parent_logits.append(bank)
+
+        child_logits = []
+        for b in range(BLOCKS):
+            bank = psum.tile([P, CHILDREN], F32, name="child_bank")
+            nc.tensor.matmul(bank[:], patient_cols[:, b * P : (b + 1) * P], child_weights[:], start=True, stop=True)
+            child_logits.append(bank)
+
+        parent_probs = []
+        for b in range(BLOCKS):
+            parent_prob = work.tile([P, CHILDREN], F32, name="parent_prob")
+            nc.scalar.activation(parent_prob[:], parent_logits[b][:], SIGMOID)
+            parent_probs.append(parent_prob)
+
+        for b in range(BLOCKS):
+            biased = work.tile([P, CHILDREN], F32, name="biased")
+            nc.vector.tensor_tensor(biased[:], child_logits[b][:], bias_rows[:], ADD)
+            child_prob = work.tile([P, CHILDREN], F32, name="child_prob")
+            nc.scalar.activation(child_prob[:], biased[:], SIGMOID)
+            joint = work.tile([P, CHILDREN], F32, name="joint")
+            nc.vector.tensor_tensor(joint[:], child_prob[:], parent_probs[b][:], MULT)
+            nc.sync.dma_start(out[b * P : (b + 1) * P, :], joint[:])

@@ -12,6 +12,7 @@ BLOCKS = PATIENTS // P
 PIECE = PARENTS
 PIECES = CHILDREN // PIECE
 PIECE_COLS = PIECE // 16
+WARMUPS = 6
 
 FLOPS = 2 * P * PATIENTS * CHILDREN * 2
 
@@ -21,8 +22,16 @@ def tile_hierarchicaldecoder_kernel(tc, w_parent, patients, w_child, b_child, of
     with (
         tc.tile_pool(name="held", bufs=1) as held,
         tc.tile_pool(name="work", bufs=BLOCKS) as work,
-        tc.psum_pool(name="psum", bufs=BLOCKS) as psum,
+        tc.psum_pool(name="parent_psum", bufs=BLOCKS) as parent_psum,
+        tc.psum_pool(name="child_psum", bufs=BLOCKS - 1) as child_psum,
+        tc.psum_pool(name="warm_psum", bufs=1) as warm_psum,
     ):
+        zeros = held.tile([P, CHILDREN], BF16, name="zeros")
+        nc.vector.memset(zeros[:], 0.0)
+        warm_bank = warm_psum.tile([P, CHILDREN], F32, name="warm_bank")
+        for warmup in range(WARMUPS):
+            nc.tensor.matmul(warm_bank[:], zeros[:, :P], zeros[:], start=True, stop=True)
+
         offsets = held.tile([P, CHILDREN // 16], U16, name="offsets")
         nc.sync.dma_start(offsets[:], offs)
         patient_cols = held.tile([P, PATIENTS], BF16, name="patient_cols")
@@ -36,7 +45,7 @@ def tile_hierarchicaldecoder_kernel(tc, w_parent, patients, w_child, b_child, of
 
         parent_logits = []
         for b in range(BLOCKS):
-            bank = psum.tile([P, CHILDREN], F32, name="parent_bank")
+            bank = parent_psum.tile([P, CHILDREN], F32, name="parent_bank")
             for piece in range(PIECES):
                 nc.tensor.matmul(
                     bank[:, piece * PIECE : (piece + 1) * PIECE],
@@ -49,7 +58,7 @@ def tile_hierarchicaldecoder_kernel(tc, w_parent, patients, w_child, b_child, of
 
         child_logits = []
         for b in range(BLOCKS):
-            bank = psum.tile([P, CHILDREN], F32, name="child_bank")
+            bank = child_psum.tile([P, CHILDREN], F32, name="child_bank")
             nc.tensor.matmul(bank[:], patient_cols[:, b * P : (b + 1) * P], child_weights[:], start=True, stop=True)
             child_logits.append(bank)
 

@@ -12,7 +12,6 @@ BLOCKS = PATIENTS // P
 PIECE = PARENTS
 PIECES = CHILDREN // PIECE
 PIECE_COLS = PIECE // 16
-WARMUPS = 6
 
 FLOPS = 2 * P * PATIENTS * CHILDREN * 2
 
@@ -22,16 +21,8 @@ def tile_hierarchicaldecoder_kernel(tc, w_parent, patients, w_child, b_child, of
     with (
         tc.tile_pool(name="held", bufs=1) as held,
         tc.tile_pool(name="work", bufs=BLOCKS) as work,
-        tc.psum_pool(name="parent_psum", bufs=BLOCKS) as parent_psum,
-        tc.psum_pool(name="child_psum", bufs=BLOCKS - 1) as child_psum,
-        tc.psum_pool(name="warm_psum", bufs=1) as warm_psum,
+        tc.psum_pool(name="psum", bufs=BLOCKS) as psum,
     ):
-        zeros = held.tile([P, CHILDREN], BF16, name="zeros")
-        nc.vector.memset(zeros[:], 0.0)
-        warm_bank = warm_psum.tile([P, CHILDREN], F32, name="warm_bank")
-        for warmup in range(WARMUPS):
-            nc.tensor.matmul(warm_bank[:], zeros[:, :P], zeros[:], start=True, stop=True)
-
         offsets = held.tile([P, CHILDREN // 16], U16, name="offsets")
         nc.sync.dma_start(offsets[:], offs)
         patient_cols = held.tile([P, PATIENTS], BF16, name="patient_cols")
@@ -41,11 +32,11 @@ def tile_hierarchicaldecoder_kernel(tc, w_parent, patients, w_child, b_child, of
         child_weights = held.tile([P, CHILDREN], BF16, name="child_weights")
         nc.scalar.dma_start(child_weights[:], w_child)
         bias_rows = held.tile([P, CHILDREN], F32, name="bias_rows")
-        nc.gpsimd.dma_start(bias_rows[:], b_child.broadcast_to([P, CHILDREN]))
+        nc.sync.dma_start(bias_rows[:], b_child.broadcast_to([P, CHILDREN]))
 
         parent_logits = []
         for b in range(BLOCKS):
-            bank = parent_psum.tile([P, CHILDREN], F32, name="parent_bank")
+            bank = psum.tile([P, CHILDREN], F32, name="parent_bank")
             for piece in range(PIECES):
                 nc.tensor.matmul(
                     bank[:, piece * PIECE : (piece + 1) * PIECE],
@@ -58,7 +49,7 @@ def tile_hierarchicaldecoder_kernel(tc, w_parent, patients, w_child, b_child, of
 
         child_logits = []
         for b in range(BLOCKS):
-            bank = child_psum.tile([P, CHILDREN], F32, name="child_bank")
+            bank = psum.tile([P, CHILDREN], F32, name="child_bank")
             nc.tensor.matmul(bank[:], patient_cols[:, b * P : (b + 1) * P], child_weights[:], start=True, stop=True)
             child_logits.append(bank)
 

@@ -27,43 +27,43 @@ def tile_hierarchicaldecoder_kernel(tc, w_parent, patients, w_child, b_child, of
         nc.sync.dma_start(offsets[:], offs)
         patient_cols = held.tile([P, PATIENTS], BF16, name="patient_cols")
         nc.scalar.dma_start(patient_cols[:], patients)
+        child_weights = held.tile([P, CHILDREN], BF16, name="child_weights")
+        nc.sync.dma_start(child_weights[:], w_child)
+        bias_rows = held.tile([P, CHILDREN], F32, name="bias_rows")
+        nc.scalar.dma_start(bias_rows[:], b_child.broadcast_to([P, CHILDREN]))
         parent_table = held.tile([P, PARENTS], BF16, name="parent_table")
         nc.sync.dma_start(parent_table[:], w_parent)
-        child_weights = held.tile([P, CHILDREN], BF16, name="child_weights")
-        nc.scalar.dma_start(child_weights[:], w_child)
-        bias_rows = held.tile([P, CHILDREN], F32, name="bias_rows")
-        nc.sync.dma_start(bias_rows[:], b_child.broadcast_to([P, CHILDREN]))
 
-        parent_logits = []
+        child_banks = []
         for b in range(BLOCKS):
-            bank = psum.tile([P, CHILDREN], F32, name="parent_bank")
+            child_bank = psum.tile([P, CHILDREN], F32, name="child_bank")
+            nc.tensor.matmul(child_bank[:], patient_cols[:, b * P : (b + 1) * P], child_weights[:], start=True, stop=True)
+            child_banks.append(child_bank)
+
+        parent_banks = []
+        for b in range(BLOCKS):
+            parent_bank = psum.tile([P, CHILDREN], F32, name="parent_bank")
             for piece in range(PIECES):
                 nc.tensor.matmul(
-                    bank[:, piece * PIECE : (piece + 1) * PIECE],
+                    parent_bank[:, piece * PIECE : (piece + 1) * PIECE],
                     patient_cols[:, b * P : (b + 1) * P],
                     parent_table[:].indirect(offsets[:, piece * PIECE_COLS : (piece + 1) * PIECE_COLS]),
                     start=True,
                     stop=True,
                 )
-            parent_logits.append(bank)
+            parent_banks.append(parent_bank)
 
-        child_logits = []
-        for b in range(BLOCKS):
-            bank = psum.tile([P, CHILDREN], F32, name="child_bank")
-            nc.tensor.matmul(bank[:], patient_cols[:, b * P : (b + 1) * P], child_weights[:], start=True, stop=True)
-            child_logits.append(bank)
-
-        parent_probs = []
-        for b in range(BLOCKS):
-            parent_prob = work.tile([P, CHILDREN], F32, name="parent_prob")
-            nc.scalar.activation(parent_prob[:], parent_logits[b][:], SIGMOID)
-            parent_probs.append(parent_prob)
-
+        child_probs = []
         for b in range(BLOCKS):
             biased = work.tile([P, CHILDREN], F32, name="biased")
-            nc.vector.tensor_tensor(biased[:], child_logits[b][:], bias_rows[:], ADD)
+            nc.vector.tensor_tensor(biased[:], child_banks[b][:], bias_rows[:], ADD)
             child_prob = work.tile([P, CHILDREN], F32, name="child_prob")
             nc.scalar.activation(child_prob[:], biased[:], SIGMOID)
+            child_probs.append(child_prob)
+
+        for b in range(BLOCKS):
+            parent_prob = work.tile([P, CHILDREN], F32, name="parent_prob")
+            nc.scalar.activation(parent_prob[:], parent_banks[b][:], SIGMOID)
             joint = work.tile([P, CHILDREN], F32, name="joint")
-            nc.vector.tensor_tensor(joint[:], child_prob[:], parent_probs[b][:], MULT)
+            nc.vector.tensor_tensor(joint[:], child_probs[b][:], parent_prob[:], MULT)
             nc.sync.dma_start(out[b * P : (b + 1) * P, :], joint[:])

@@ -12,6 +12,7 @@ BLOCKS = PATIENTS // P
 PIECE = PARENTS
 PIECES = CHILDREN // PIECE
 PIECE_COLS = PIECE // 16
+SQUARE = 32
 
 FLOPS = 2 * P * PATIENTS * CHILDREN * 2
 
@@ -27,43 +28,54 @@ def tile_hierarchicaldecoder_kernel(tc, w_parent, patients, w_child, b_child, of
         nc.sync.dma_start(offsets[:], offs)
         patient_cols = held.tile([P, PATIENTS], BF16, name="patient_cols")
         nc.scalar.dma_start(patient_cols[:], patients)
-        child_weights = held.tile([P, CHILDREN], BF16, name="child_weights")
-        nc.sync.dma_start(child_weights[:], w_child)
-        bias_rows = held.tile([P, CHILDREN], F32, name="bias_rows")
-        nc.scalar.dma_start(bias_rows[:], b_child.broadcast_to([P, CHILDREN]))
         parent_table = held.tile([P, PARENTS], BF16, name="parent_table")
         nc.sync.dma_start(parent_table[:], w_parent)
+        child_weights = held.tile([P, CHILDREN], BF16, name="child_weights")
+        nc.scalar.dma_start(child_weights[:], w_child)
+        bias_seed = held.tile([P, CHILDREN], F32, name="bias_seed", align_bytes=64)
+        nc.gpsimd.memset(bias_seed[:], 0.0)
+        for a in range(P // SQUARE):
+            nc.sync.dma_start(bias_seed[a * SQUARE : a * SQUARE + 1, :], b_child)
+        bias_cols = held.tile([P, CHILDREN], F32, name="bias_cols", align_bytes=64)
+        nc.vector.transpose(bias_cols[:], bias_seed[:])
+        bias_wide = held.tile([P, CHILDREN], F32, name="bias_wide", align_bytes=64)
+        nc.vector.tensor_copy(
+            bias_wide[:].rearrange("p (c k) -> p c k", k=SQUARE),
+            bias_cols[:].rearrange("p (c k) -> p c k", k=SQUARE)[:, :, 0:1].to_broadcast([P, CHILDREN // SQUARE, SQUARE]),
+        )
+        bias_rows = held.tile([P, CHILDREN], F32, name="bias_rows", align_bytes=64)
+        nc.vector.transpose(bias_rows[:], bias_wide[:])
 
-        child_banks = []
+        parent_logits = []
         for b in range(BLOCKS):
-            child_bank = psum.tile([P, CHILDREN], F32, name="child_bank")
-            nc.tensor.matmul(child_bank[:], patient_cols[:, b * P : (b + 1) * P], child_weights[:], start=True, stop=True)
-            child_banks.append(child_bank)
-
-        parent_banks = []
-        for b in range(BLOCKS):
-            parent_bank = psum.tile([P, CHILDREN], F32, name="parent_bank")
+            bank = psum.tile([P, CHILDREN], F32, name="parent_bank")
             for piece in range(PIECES):
                 nc.tensor.matmul(
-                    parent_bank[:, piece * PIECE : (piece + 1) * PIECE],
+                    bank[:, piece * PIECE : (piece + 1) * PIECE],
                     patient_cols[:, b * P : (b + 1) * P],
                     parent_table[:].indirect(offsets[:, piece * PIECE_COLS : (piece + 1) * PIECE_COLS]),
                     start=True,
                     stop=True,
                 )
-            parent_banks.append(parent_bank)
+            parent_logits.append(bank)
 
-        child_probs = []
+        child_logits = []
         for b in range(BLOCKS):
-            biased = work.tile([P, CHILDREN], F32, name="biased")
-            nc.vector.tensor_tensor(biased[:], child_banks[b][:], bias_rows[:], ADD)
-            child_prob = work.tile([P, CHILDREN], F32, name="child_prob")
-            nc.scalar.activation(child_prob[:], biased[:], SIGMOID)
-            child_probs.append(child_prob)
+            bank = psum.tile([P, CHILDREN], F32, name="child_bank")
+            nc.tensor.matmul(bank[:], patient_cols[:, b * P : (b + 1) * P], child_weights[:], start=True, stop=True)
+            child_logits.append(bank)
 
+        parent_probs = []
         for b in range(BLOCKS):
             parent_prob = work.tile([P, CHILDREN], F32, name="parent_prob")
-            nc.scalar.activation(parent_prob[:], parent_banks[b][:], SIGMOID)
+            nc.scalar.activation(parent_prob[:], parent_logits[b][:], SIGMOID)
+            parent_probs.append(parent_prob)
+
+        for b in range(BLOCKS):
+            biased = work.tile([P, CHILDREN], F32, name="biased")
+            nc.vector.tensor_tensor(biased[:], child_logits[b][:], bias_rows[:], ADD)
+            child_prob = work.tile([P, CHILDREN], F32, name="child_prob")
+            nc.scalar.activation(child_prob[:], biased[:], SIGMOID)
             joint = work.tile([P, CHILDREN], F32, name="joint")
-            nc.vector.tensor_tensor(joint[:], child_probs[b][:], parent_prob[:], MULT)
+            nc.vector.tensor_tensor(joint[:], child_prob[:], parent_probs[b][:], MULT)
             nc.sync.dma_start(out[b * P : (b + 1) * P, :], joint[:])

@@ -24,58 +24,64 @@ def tile_hierarchicaldecoder_kernel(tc, w_parent, patients, w_child, b_child, of
         tc.tile_pool(name="work", bufs=BLOCKS) as work,
         tc.psum_pool(name="psum", bufs=BLOCKS) as psum,
     ):
-        offsets = held.tile([P, CHILDREN // 16], U16, name="offsets")
-        nc.sync.dma_start(offsets[:], offs)
+        bias_square = held.tile([P, SQUARE], F32, name="bias_square", align_bytes=64)
+        nc.gpsimd.memset(bias_square[:], 0.0)
+        for a in range(P // SQUARE):
+            queue = nc.sync if a % 2 == 0 else nc.scalar
+            queue.dma_start(
+                bias_square[a * SQUARE : a * SQUARE + CHILDREN // SQUARE, :],
+                b_child.rearrange("o (c k) -> (o c) k", k=SQUARE),
+            )
+
         patient_cols = held.tile([P, PATIENTS], BF16, name="patient_cols")
         nc.scalar.dma_start(patient_cols[:], patients)
-        parent_table = held.tile([P, PARENTS], BF16, name="parent_table")
-        nc.sync.dma_start(parent_table[:], w_parent)
         child_weights = held.tile([P, CHILDREN], BF16, name="child_weights")
-        nc.scalar.dma_start(child_weights[:], w_child)
-        bias_seed = held.tile([P, CHILDREN], F32, name="bias_seed", align_bytes=64)
-        nc.gpsimd.memset(bias_seed[:], 0.0)
-        for a in range(P // SQUARE):
-            nc.sync.dma_start(bias_seed[a * SQUARE : a * SQUARE + 1, :], b_child)
-        bias_cols = held.tile([P, CHILDREN], F32, name="bias_cols", align_bytes=64)
-        nc.vector.transpose(bias_cols[:], bias_seed[:])
+        nc.sync.dma_start(child_weights[:], w_child)
+        offsets = held.tile([P, CHILDREN // 16], U16, name="offsets")
+        nc.sync.dma_start(offsets[:], offs)
+        parent_table = held.tile([P, PARENTS], BF16, name="parent_table")
+        nc.scalar.dma_start(parent_table[:], w_parent)
+
+        bias_cols = held.tile([P, SQUARE], F32, name="bias_cols", align_bytes=64)
+        nc.vector.transpose(bias_cols[:], bias_square[:])
         bias_wide = held.tile([P, CHILDREN], F32, name="bias_wide", align_bytes=64)
         nc.vector.tensor_copy(
             bias_wide[:].rearrange("p (c k) -> p c k", k=SQUARE),
-            bias_cols[:].rearrange("p (c k) -> p c k", k=SQUARE)[:, :, 0:1].to_broadcast([P, CHILDREN // SQUARE, SQUARE]),
+            bias_cols[:, : CHILDREN // SQUARE].unsqueeze(2).to_broadcast([P, CHILDREN // SQUARE, SQUARE]),
         )
         bias_rows = held.tile([P, CHILDREN], F32, name="bias_rows", align_bytes=64)
         nc.vector.transpose(bias_rows[:], bias_wide[:])
 
-        parent_logits = []
+        child_banks = []
         for b in range(BLOCKS):
-            bank = psum.tile([P, CHILDREN], F32, name="parent_bank")
+            child_bank = psum.tile([P, CHILDREN], F32, name="child_bank")
+            nc.tensor.matmul(child_bank[:], patient_cols[:, b * P : (b + 1) * P], child_weights[:], start=True, stop=True)
+            child_banks.append(child_bank)
+
+        parent_banks = []
+        for b in range(BLOCKS):
+            parent_bank = psum.tile([P, CHILDREN], F32, name="parent_bank")
             for piece in range(PIECES):
                 nc.tensor.matmul(
-                    bank[:, piece * PIECE : (piece + 1) * PIECE],
+                    parent_bank[:, piece * PIECE : (piece + 1) * PIECE],
                     patient_cols[:, b * P : (b + 1) * P],
                     parent_table[:].indirect(offsets[:, piece * PIECE_COLS : (piece + 1) * PIECE_COLS]),
                     start=True,
                     stop=True,
                 )
-            parent_logits.append(bank)
+            parent_banks.append(parent_bank)
 
-        child_logits = []
+        child_probs = []
         for b in range(BLOCKS):
-            bank = psum.tile([P, CHILDREN], F32, name="child_bank")
-            nc.tensor.matmul(bank[:], patient_cols[:, b * P : (b + 1) * P], child_weights[:], start=True, stop=True)
-            child_logits.append(bank)
-
-        parent_probs = []
-        for b in range(BLOCKS):
-            parent_prob = work.tile([P, CHILDREN], F32, name="parent_prob")
-            nc.scalar.activation(parent_prob[:], parent_logits[b][:], SIGMOID)
-            parent_probs.append(parent_prob)
-
-        for b in range(BLOCKS):
-            biased = work.tile([P, CHILDREN], F32, name="biased")
-            nc.vector.tensor_tensor(biased[:], child_logits[b][:], bias_rows[:], ADD)
+            biased = work.tile([P, CHILDREN], F32, name="biased", tag="scalar_side")
+            nc.vector.tensor_tensor(biased[:], child_banks[b][:], bias_rows[:], ADD)
             child_prob = work.tile([P, CHILDREN], F32, name="child_prob")
             nc.scalar.activation(child_prob[:], biased[:], SIGMOID)
+            child_probs.append(child_prob)
+
+        for b in range(BLOCKS):
+            parent_prob = work.tile([P, CHILDREN], F32, name="parent_prob", tag="scalar_side")
+            nc.scalar.activation(parent_prob[:], parent_banks[b][:], SIGMOID)
             joint = work.tile([P, CHILDREN], F32, name="joint")
-            nc.vector.tensor_tensor(joint[:], child_prob[:], parent_probs[b][:], MULT)
+            nc.vector.tensor_tensor(joint[:], child_probs[b][:], parent_prob[:], MULT)
             nc.sync.dma_start(out[b * P : (b + 1) * P, :], joint[:])

@@ -13,6 +13,7 @@ PIECE = PARENTS
 PIECES = CHILDREN // PIECE
 PIECE_COLS = PIECE // 16
 SQUARE = 32
+WARMUPS = 4
 
 FLOPS = 2 * P * PATIENTS * CHILDREN * 2
 
@@ -24,6 +25,21 @@ def tile_hierarchicaldecoder_kernel(tc, w_parent, patients, w_child, b_child, of
         tc.tile_pool(name="work", bufs=BLOCKS) as work,
         tc.psum_pool(name="psum", bufs=BLOCKS) as psum,
     ):
+        zeros = held.tile([P, CHILDREN], BF16, name="zeros")
+        nc.vector.memset(zeros[:], 0.0)
+        warm_bank = psum.tile([P, CHILDREN], F32, name="warm_bank", tag="child_bank")
+        for warmup in range(WARMUPS):
+            nc.tensor.matmul(warm_bank[:], zeros[:, :P], zeros[:], start=True, stop=True)
+
+        offsets = held.tile([P, CHILDREN // 16], U16, name="offsets")
+        nc.sync.dma_start(offsets[:], offs)
+        patient_cols = held.tile([P, PATIENTS], BF16, name="patient_cols")
+        nc.scalar.dma_start(patient_cols[:], patients)
+        parent_table = held.tile([P, PARENTS], BF16, name="parent_table")
+        nc.sync.dma_start(parent_table[:], w_parent)
+        child_weights = held.tile([P, CHILDREN], BF16, name="child_weights")
+        nc.scalar.dma_start(child_weights[:], w_child)
+
         bias_square = held.tile([P, SQUARE], F32, name="bias_square", align_bytes=64)
         nc.gpsimd.memset(bias_square[:], 0.0)
         for a in range(P // SQUARE):
@@ -32,16 +48,6 @@ def tile_hierarchicaldecoder_kernel(tc, w_parent, patients, w_child, b_child, of
                 bias_square[a * SQUARE : a * SQUARE + CHILDREN // SQUARE, :],
                 b_child.rearrange("o (c k) -> (o c) k", k=SQUARE),
             )
-
-        patient_cols = held.tile([P, PATIENTS], BF16, name="patient_cols")
-        nc.scalar.dma_start(patient_cols[:], patients)
-        child_weights = held.tile([P, CHILDREN], BF16, name="child_weights")
-        nc.sync.dma_start(child_weights[:], w_child)
-        offsets = held.tile([P, CHILDREN // 16], U16, name="offsets")
-        nc.sync.dma_start(offsets[:], offs)
-        parent_table = held.tile([P, PARENTS], BF16, name="parent_table")
-        nc.scalar.dma_start(parent_table[:], w_parent)
-
         bias_cols = held.tile([P, SQUARE], F32, name="bias_cols", align_bytes=64)
         nc.vector.transpose(bias_cols[:], bias_square[:])
         bias_wide = held.tile([P, CHILDREN], F32, name="bias_wide", align_bytes=64)
@@ -51,12 +57,6 @@ def tile_hierarchicaldecoder_kernel(tc, w_parent, patients, w_child, b_child, of
         )
         bias_rows = held.tile([P, CHILDREN], F32, name="bias_rows", align_bytes=64)
         nc.vector.transpose(bias_rows[:], bias_wide[:])
-
-        child_banks = []
-        for b in range(BLOCKS):
-            child_bank = psum.tile([P, CHILDREN], F32, name="child_bank")
-            nc.tensor.matmul(child_bank[:], patient_cols[:, b * P : (b + 1) * P], child_weights[:], start=True, stop=True)
-            child_banks.append(child_bank)
 
         parent_banks = []
         for b in range(BLOCKS):
@@ -71,17 +71,28 @@ def tile_hierarchicaldecoder_kernel(tc, w_parent, patients, w_child, b_child, of
                 )
             parent_banks.append(parent_bank)
 
+        child_banks = []
+        for b in range(BLOCKS):
+            child_bank = psum.tile([P, CHILDREN], F32, name="child_bank")
+            nc.tensor.matmul(child_bank[:], patient_cols[:, b * P : (b + 1) * P], child_weights[:], start=True, stop=True)
+            child_banks.append(child_bank)
+
+        parent_probs = []
+        for b in range(BLOCKS):
+            parent_prob = work.tile([P, CHILDREN], F32, name="parent_prob")
+            nc.scalar.activation(parent_prob[:], parent_banks[b][:], SIGMOID)
+            parent_probs.append(parent_prob)
+
         child_probs = []
         for b in range(BLOCKS):
-            biased = work.tile([P, CHILDREN], F32, name="biased", tag="scalar_side")
+            biased = work.tile([P, CHILDREN], F32, name="biased")
             nc.vector.tensor_tensor(biased[:], child_banks[b][:], bias_rows[:], ADD)
             child_prob = work.tile([P, CHILDREN], F32, name="child_prob")
             nc.scalar.activation(child_prob[:], biased[:], SIGMOID)
             child_probs.append(child_prob)
 
         for b in range(BLOCKS):
-            parent_prob = work.tile([P, CHILDREN], F32, name="parent_prob", tag="scalar_side")
-            nc.scalar.activation(parent_prob[:], parent_banks[b][:], SIGMOID)
+            multiplier = nc.gpsimd if b == 0 else nc.vector
             joint = work.tile([P, CHILDREN], F32, name="joint")
-            nc.vector.tensor_tensor(joint[:], child_probs[b][:], parent_prob[:], MULT)
+            multiplier.tensor_tensor(joint[:], child_probs[b][:], parent_probs[b][:], MULT)
             nc.sync.dma_start(out[b * P : (b + 1) * P, :], joint[:])

@@ -12,7 +12,8 @@ BLOCKS = PATIENTS // P
 PIECE = PARENTS
 PIECES = CHILDREN // PIECE
 PIECE_COLS = PIECE // 16
-SQUARE = 32
+TERMS = 3
+TERM_ROWS = 4
 WARMUPS = 4
 
 FLOPS = 2 * P * PATIENTS * CHILDREN * 2
@@ -40,23 +41,28 @@ def tile_hierarchicaldecoder_kernel(tc, w_parent, patients, w_child, b_child, of
         child_weights = held.tile([P, CHILDREN], BF16, name="child_weights")
         nc.scalar.dma_start(child_weights[:], w_child)
 
-        bias_square = held.tile([P, SQUARE], F32, name="bias_square", align_bytes=64)
-        nc.gpsimd.memset(bias_square[:], 0.0)
-        for a in range(P // SQUARE):
-            queue = nc.sync if a % 2 == 0 else nc.scalar
-            queue.dma_start(
-                bias_square[a * SQUARE : a * SQUARE + CHILDREN // SQUARE, :],
-                b_child.rearrange("o (c k) -> (o c) k", k=SQUARE),
-            )
-        bias_cols = held.tile([P, SQUARE], F32, name="bias_cols", align_bytes=64)
-        nc.vector.transpose(bias_cols[:], bias_square[:])
-        bias_wide = held.tile([P, CHILDREN], F32, name="bias_wide", align_bytes=64)
-        nc.vector.tensor_copy(
-            bias_wide[:].rearrange("p (c k) -> p c k", k=SQUARE),
-            bias_cols[:, : CHILDREN // SQUARE].unsqueeze(2).to_broadcast([P, CHILDREN // SQUARE, SQUARE]),
+        bias_copies = held.tile([TERM_ROWS, CHILDREN], F32, name="bias_copies")
+        nc.sync.dma_start(bias_copies[:], b_child.rearrange("o n -> (o n)").partition_broadcast(TERM_ROWS))
+        selector = held.tile([P, P], BF16, name="selector")
+        nc.gpsimd.memset(selector[:], 0.0)
+        nc.gpsimd.memset(selector[:TERMS, :], 1.0)
+        bias_terms = held.tile([P, CHILDREN], BF16, name="bias_terms")
+        nc.gpsimd.memset(bias_terms[:], 0.0)
+        minus_first = held.tile([TERM_ROWS, 1], F32, name="minus_first")
+        nc.gpsimd.memset(minus_first[:], -1.0)
+        nc.gpsimd.memset(minus_first[:1, :], 0.0)
+        minus_second = held.tile([TERM_ROWS, 1], F32, name="minus_second")
+        nc.gpsimd.memset(minus_second[:], -1.0)
+        nc.gpsimd.memset(minus_second[:2, :], 0.0)
+        first_term = held.tile([TERM_ROWS, CHILDREN], BF16, name="first_term")
+        nc.vector.tensor_copy(first_term[:], bias_copies[:])
+        left_over = held.tile([TERM_ROWS, CHILDREN], F32, name="left_over")
+        nc.vector.scalar_tensor_tensor(left_over[:], first_term[:], minus_first[:, 0:1], bias_copies[:], MULT, ADD)
+        second_term = held.tile([TERM_ROWS, CHILDREN], BF16, name="second_term")
+        nc.vector.tensor_copy(second_term[:], left_over[:])
+        nc.vector.scalar_tensor_tensor(
+            bias_terms[:TERM_ROWS, :], second_term[:], minus_second[:, 0:1], left_over[:], MULT, ADD
         )
-        bias_rows = held.tile([P, CHILDREN], F32, name="bias_rows", align_bytes=64)
-        nc.vector.transpose(bias_rows[:], bias_wide[:])
 
         parent_banks = []
         for b in range(BLOCKS):
@@ -74,7 +80,8 @@ def tile_hierarchicaldecoder_kernel(tc, w_parent, patients, w_child, b_child, of
         child_banks = []
         for b in range(BLOCKS):
             child_bank = psum.tile([P, CHILDREN], F32, name="child_bank")
-            nc.tensor.matmul(child_bank[:], patient_cols[:, b * P : (b + 1) * P], child_weights[:], start=True, stop=True)
+            nc.tensor.matmul(child_bank[:], patient_cols[:, b * P : (b + 1) * P], child_weights[:], start=True, stop=False)
+            nc.tensor.matmul(child_bank[:], selector[:], bias_terms[:], start=False, stop=True)
             child_banks.append(child_bank)
 
         parent_probs = []
@@ -83,16 +90,9 @@ def tile_hierarchicaldecoder_kernel(tc, w_parent, patients, w_child, b_child, of
             nc.scalar.activation(parent_prob[:], parent_banks[b][:], SIGMOID)
             parent_probs.append(parent_prob)
 
-        child_probs = []
         for b in range(BLOCKS):
-            biased = work.tile([P, CHILDREN], F32, name="biased")
-            nc.vector.tensor_tensor(biased[:], child_banks[b][:], bias_rows[:], ADD)
             child_prob = work.tile([P, CHILDREN], F32, name="child_prob")
-            nc.scalar.activation(child_prob[:], biased[:], SIGMOID)
-            child_probs.append(child_prob)
-
-        for b in range(BLOCKS):
-            multiplier = nc.gpsimd if b == 0 else nc.vector
+            nc.scalar.activation(child_prob[:], child_banks[b][:], SIGMOID)
             joint = work.tile([P, CHILDREN], F32, name="joint")
-            multiplier.tensor_tensor(joint[:], child_probs[b][:], parent_probs[b][:], MULT)
+            nc.vector.tensor_tensor(joint[:], child_prob[:], parent_probs[b][:], MULT)
             nc.sync.dma_start(out[b * P : (b + 1) * P, :], joint[:])

@@ -13,7 +13,6 @@ PIECE = PARENTS
 PIECES = CHILDREN // PIECE
 PIECE_COLS = PIECE // 16
 TERMS = 3
-TERM_ROWS = 4
 WARMUPS = 4
 
 FLOPS = 2 * P * PATIENTS * CHILDREN * 2
@@ -41,27 +40,29 @@ def tile_hierarchicaldecoder_kernel(tc, w_parent, patients, w_child, b_child, of
         child_weights = held.tile([P, CHILDREN], BF16, name="child_weights")
         nc.scalar.dma_start(child_weights[:], w_child)
 
-        bias_copies = held.tile([TERM_ROWS, CHILDREN], F32, name="bias_copies")
-        nc.sync.dma_start(bias_copies[:], b_child.rearrange("o n -> (o n)").partition_broadcast(TERM_ROWS))
+        bias_copies = held.tile([TERMS, CHILDREN], F32, name="bias_copies")
+        for term in range(TERMS):
+            queue = nc.sync if term % 2 == 0 else nc.scalar
+            queue.dma_start(bias_copies[term : term + 1, :], b_child)
         selector = held.tile([P, P], BF16, name="selector")
         nc.gpsimd.memset(selector[:], 0.0)
         nc.gpsimd.memset(selector[:TERMS, :], 1.0)
         bias_terms = held.tile([P, CHILDREN], BF16, name="bias_terms")
         nc.gpsimd.memset(bias_terms[:], 0.0)
-        minus_first = held.tile([TERM_ROWS, 1], F32, name="minus_first")
+        minus_first = held.tile([TERMS, 1], F32, name="minus_first")
         nc.gpsimd.memset(minus_first[:], -1.0)
         nc.gpsimd.memset(minus_first[:1, :], 0.0)
-        minus_second = held.tile([TERM_ROWS, 1], F32, name="minus_second")
+        minus_second = held.tile([TERMS, 1], F32, name="minus_second")
         nc.gpsimd.memset(minus_second[:], -1.0)
         nc.gpsimd.memset(minus_second[:2, :], 0.0)
-        first_term = held.tile([TERM_ROWS, CHILDREN], BF16, name="first_term")
+        first_term = held.tile([TERMS, CHILDREN], BF16, name="first_term")
         nc.vector.tensor_copy(first_term[:], bias_copies[:])
-        left_over = held.tile([TERM_ROWS, CHILDREN], F32, name="left_over")
+        left_over = held.tile([TERMS, CHILDREN], F32, name="left_over")
         nc.vector.scalar_tensor_tensor(left_over[:], first_term[:], minus_first[:, 0:1], bias_copies[:], MULT, ADD)
-        second_term = held.tile([TERM_ROWS, CHILDREN], BF16, name="second_term")
+        second_term = held.tile([TERMS, CHILDREN], BF16, name="second_term")
         nc.vector.tensor_copy(second_term[:], left_over[:])
         nc.vector.scalar_tensor_tensor(
-            bias_terms[:TERM_ROWS, :], second_term[:], minus_second[:, 0:1], left_over[:], MULT, ADD
+            bias_terms[:TERMS, :], second_term[:], minus_second[:, 0:1], left_over[:], MULT, ADD
         )
 
         parent_banks = []
@@ -80,8 +81,8 @@ def tile_hierarchicaldecoder_kernel(tc, w_parent, patients, w_child, b_child, of
         child_banks = []
         for b in range(BLOCKS):
             child_bank = psum.tile([P, CHILDREN], F32, name="child_bank")
-            nc.tensor.matmul(child_bank[:], patient_cols[:, b * P : (b + 1) * P], child_weights[:], start=True, stop=False)
-            nc.tensor.matmul(child_bank[:], selector[:], bias_terms[:], start=False, stop=True)
+            nc.tensor.matmul(child_bank[:], selector[:], bias_terms[:], start=True, stop=False)
+            nc.tensor.matmul(child_bank[:], patient_cols[:, b * P : (b + 1) * P], child_weights[:], start=False, stop=True)
             child_banks.append(child_bank)
 
         parent_probs = []

@@ -1,8 +1,8 @@
 import concourse.mybir as mybir
 
-BF16, F32, U16 = mybir.dt.bfloat16, mybir.dt.float32, mybir.dt.uint16
+BF16, F32, U16, I32 = mybir.dt.bfloat16, mybir.dt.float32, mybir.dt.uint16, mybir.dt.int32
 SIGMOID = mybir.ActivationFunctionType.Sigmoid
-ADD, MULT = mybir.AluOpType.add, mybir.AluOpType.mult
+MULT, SUBTRACT, AND = mybir.AluOpType.mult, mybir.AluOpType.subtract, mybir.AluOpType.bitwise_and
 
 P = 128
 PARENTS = 256
@@ -12,7 +12,10 @@ BLOCKS = PATIENTS // P
 PIECE = PARENTS
 PIECES = CHILDREN // PIECE
 PIECE_COLS = PIECE // 16
-TERMS = 3
+TOP_8, TOP_16, ALL_24 = -(1 << 16), -(1 << 8), -1
+KEEP = (TOP_8, TOP_16, ALL_24)
+DROP = (0, TOP_8, TOP_16)
+TERMS = len(KEEP)
 WARMUPS = 4
 
 FLOPS = 2 * P * PATIENTS * CHILDREN * 2
@@ -44,26 +47,21 @@ def tile_hierarchicaldecoder_kernel(tc, w_parent, patients, w_child, b_child, of
         for term in range(TERMS):
             queue = nc.sync if term % 2 == 0 else nc.scalar
             queue.dma_start(bias_copies[term : term + 1, :], b_child)
+        keep_mask = held.tile([TERMS, 1], I32, name="keep_mask")
+        drop_mask = held.tile([TERMS, 1], I32, name="drop_mask")
+        for term in reversed(range(TERMS)):
+            nc.vector.memset(keep_mask[: term + 1, :], KEEP[term])
+            nc.vector.memset(drop_mask[: term + 1, :], DROP[term])
         selector = held.tile([P, P], BF16, name="selector")
-        nc.gpsimd.memset(selector[:], 0.0)
-        nc.gpsimd.memset(selector[:TERMS, :], 1.0)
+        nc.vector.memset(selector[:], 0.0)
+        nc.vector.memset(selector[:TERMS, :], 1.0)
         bias_terms = held.tile([P, CHILDREN], BF16, name="bias_terms")
-        nc.gpsimd.memset(bias_terms[:], 0.0)
-        minus_first = held.tile([TERMS, 1], F32, name="minus_first")
-        nc.gpsimd.memset(minus_first[:], -1.0)
-        nc.gpsimd.memset(minus_first[:1, :], 0.0)
-        minus_second = held.tile([TERMS, 1], F32, name="minus_second")
-        nc.gpsimd.memset(minus_second[:], -1.0)
-        nc.gpsimd.memset(minus_second[:2, :], 0.0)
-        first_term = held.tile([TERMS, CHILDREN], BF16, name="first_term")
-        nc.vector.tensor_copy(first_term[:], bias_copies[:])
-        left_over = held.tile([TERMS, CHILDREN], F32, name="left_over")
-        nc.vector.scalar_tensor_tensor(left_over[:], first_term[:], minus_first[:, 0:1], bias_copies[:], MULT, ADD)
-        second_term = held.tile([TERMS, CHILDREN], BF16, name="second_term")
-        nc.vector.tensor_copy(second_term[:], left_over[:])
-        nc.vector.scalar_tensor_tensor(
-            bias_terms[:TERMS, :], second_term[:], minus_second[:, 0:1], left_over[:], MULT, ADD
-        )
+        nc.vector.memset(bias_terms[:], 0.0)
+        kept = held.tile([TERMS, CHILDREN], I32, name="kept")
+        nc.vector.tensor_scalar(kept[:], bias_copies[:].bitcast(I32), keep_mask[:, 0:1], None, AND)
+        dropped = held.tile([TERMS, CHILDREN], I32, name="dropped")
+        nc.vector.tensor_scalar(dropped[:], bias_copies[:].bitcast(I32), drop_mask[:, 0:1], None, AND)
+        nc.vector.tensor_tensor(bias_terms[:TERMS, :], kept[:].bitcast(F32), dropped[:].bitcast(F32), SUBTRACT)
 
         parent_banks = []
         for b in range(BLOCKS):

@@ -16,7 +16,7 @@ TOP_8, TOP_16, ALL_24 = -(1 << 16), -(1 << 8), -1
 KEEP = (TOP_8, TOP_16, ALL_24)
 DROP = (0, TOP_8, TOP_16)
 TERMS = len(KEEP)
-WARMUPS = 4
+WARMUPS = 3
 
 FLOPS = 2 * P * PATIENTS * CHILDREN * 2
 

@@ -16,6 +16,11 @@ TOP_8, TOP_16, ALL_24 = -(1 << 16), -(1 << 8), -1
 KEEP = (TOP_8, TOP_16, ALL_24)
 DROP = (0, TOP_8, TOP_16)
 TERMS = len(KEEP)
+HALVES = 2
+HALF = CHILDREN // HALVES
+BIAS_ROWS = HALVES * TERMS
+EARLY = BLOCKS // 2
+CHILD_PIECE = 128
 WARMUPS = 3
 
 FLOPS = 2 * P * PATIENTS * CHILDREN * 2
@@ -34,38 +39,65 @@ def tile_hierarchicaldecoder_kernel(tc, w_parent, patients, w_child, b_child, of
         for warmup in range(WARMUPS):
             nc.tensor.matmul(warm_bank[:], zeros[:, :P], zeros[:], start=True, stop=True)
 
+        bias_copies = held.tile([BIAS_ROWS, HALF], F32, name="bias_copies")
+        bias_halves = b_child.rearrange("o (h n) -> (o h) n", h=HALVES)
+        for term in range(TERMS):
+            nc.scalar.dma_start(bias_copies[term::TERMS, :], bias_halves)
+        patient_cols = held.tile([P, PATIENTS], BF16, name="patient_cols")
+        nc.sync.dma_start(patient_cols[:], patients)
         offsets = held.tile([P, CHILDREN // 16], U16, name="offsets")
         nc.sync.dma_start(offsets[:], offs)
-        patient_cols = held.tile([P, PATIENTS], BF16, name="patient_cols")
-        nc.scalar.dma_start(patient_cols[:], patients)
         parent_table = held.tile([P, PARENTS], BF16, name="parent_table")
         nc.sync.dma_start(parent_table[:], w_parent)
         child_weights = held.tile([P, CHILDREN], BF16, name="child_weights")
-        nc.scalar.dma_start(child_weights[:], w_child)
+        nc.sync.dma_start(child_weights[:], w_child)
 
-        bias_copies = held.tile([TERMS, CHILDREN], F32, name="bias_copies")
-        for term in range(TERMS):
-            queue = nc.sync if term % 2 == 0 else nc.scalar
-            queue.dma_start(bias_copies[term : term + 1, :], b_child)
-        keep_mask = held.tile([TERMS, 1], I32, name="keep_mask")
-        drop_mask = held.tile([TERMS, 1], I32, name="drop_mask")
-        for term in reversed(range(TERMS)):
-            nc.vector.memset(keep_mask[: term + 1, :], KEEP[term])
-            nc.vector.memset(drop_mask[: term + 1, :], DROP[term])
-        selector = held.tile([P, P], BF16, name="selector")
-        nc.vector.memset(selector[:], 0.0)
-        nc.vector.memset(selector[:TERMS, :], 1.0)
-        bias_terms = held.tile([P, CHILDREN], BF16, name="bias_terms")
+        keep_mask = held.tile([BIAS_ROWS, 1], I32, name="keep_mask")
+        drop_mask = held.tile([BIAS_ROWS, 1], I32, name="drop_mask")
+        for row in reversed(range(BIAS_ROWS)):
+            nc.vector.memset(keep_mask[: row + 1, :], KEEP[row % TERMS])
+            nc.vector.memset(drop_mask[: row + 1, :], DROP[row % TERMS])
+        selectors = held.tile([P, HALVES * P], BF16, name="selectors")
+        nc.vector.memset(selectors[:], 0.0)
+        for half in range(HALVES):
+            selector = selectors[:, half * P : (half + 1) * P]
+            nc.vector.memset(selector[: (half + 1) * TERMS, :], 1.0)
+            if half > 0:
+                nc.vector.memset(selector[: half * TERMS, :], 0.0)
+        bias_terms = held.tile([P, HALF], BF16, name="bias_terms")
         nc.vector.memset(bias_terms[:], 0.0)
-        kept = held.tile([TERMS, CHILDREN], I32, name="kept")
+        kept = held.tile([BIAS_ROWS, HALF], I32, name="kept")
         nc.vector.tensor_scalar(kept[:], bias_copies[:].bitcast(I32), keep_mask[:, 0:1], None, AND)
-        dropped = held.tile([TERMS, CHILDREN], I32, name="dropped")
+        dropped = held.tile([BIAS_ROWS, HALF], I32, name="dropped")
         nc.vector.tensor_scalar(dropped[:], bias_copies[:].bitcast(I32), drop_mask[:, 0:1], None, AND)
-        nc.vector.tensor_tensor(bias_terms[:TERMS, :], kept[:].bitcast(F32), dropped[:].bitcast(F32), SUBTRACT)
+        nc.vector.tensor_tensor(bias_terms[:BIAS_ROWS, :], kept[:].bitcast(F32), dropped[:].bitcast(F32), SUBTRACT)
 
-        parent_banks = []
-        for b in range(BLOCKS):
-            parent_bank = psum.tile([P, CHILDREN], F32, name="parent_bank")
+        child_probs, parent_probs = {}, {}
+
+        def child(b):
+            child_bank = psum.tile([P, CHILDREN], F32, name="child_bank")
+            for half in range(HALVES):
+                nc.tensor.matmul(
+                    child_bank[:, half * HALF : (half + 1) * HALF],
+                    selectors[:, half * P : (half + 1) * P],
+                    bias_terms[:],
+                    start=half == 0,
+                    stop=False,
+                )
+            for first in range(0, CHILDREN, CHILD_PIECE):
+                nc.tensor.matmul(
+                    child_bank[:, first : first + CHILD_PIECE],
+                    patient_cols[:, b * P : (b + 1) * P],
+                    child_weights[:, first : first + CHILD_PIECE],
+                    start=False,
+                    stop=first + CHILD_PIECE == CHILDREN,
+                )
+            child_prob = work.tile([P, CHILDREN], F32, name="child_prob")
+            nc.scalar.activation(child_prob[:], child_bank[:], SIGMOID)
+            child_probs[b] = child_prob
+
+        def parent(b):
+            parent_bank = psum.tile([P, CHILDREN], F32, name="parent_bank", bufs=EARLY)
             for piece in range(PIECES):
                 nc.tensor.matmul(
                     parent_bank[:, piece * PIECE : (piece + 1) * PIECE],
@@ -74,24 +106,22 @@ def tile_hierarchicaldecoder_kernel(tc, w_parent, patients, w_child, b_child, of
                     start=True,
                     stop=True,
                 )
-            parent_banks.append(parent_bank)
-
-        child_banks = []
-        for b in range(BLOCKS):
-            child_bank = psum.tile([P, CHILDREN], F32, name="child_bank")
-            nc.tensor.matmul(child_bank[:], selector[:], bias_terms[:], start=True, stop=False)
-            nc.tensor.matmul(child_bank[:], patient_cols[:, b * P : (b + 1) * P], child_weights[:], start=False, stop=True)
-            child_banks.append(child_bank)
-
-        parent_probs = []
-        for b in range(BLOCKS):
             parent_prob = work.tile([P, CHILDREN], F32, name="parent_prob")
-            nc.scalar.activation(parent_prob[:], parent_banks[b][:], SIGMOID)
-            parent_probs.append(parent_prob)
+            nc.scalar.activation(parent_prob[:], parent_bank[:], SIGMOID)
+            parent_probs[b] = parent_prob
 
-        for b in range(BLOCKS):
-            child_prob = work.tile([P, CHILDREN], F32, name="child_prob")
-            nc.scalar.activation(child_prob[:], child_banks[b][:], SIGMOID)
-            joint = work.tile([P, CHILDREN], F32, name="joint")
-            nc.vector.tensor_tensor(joint[:], child_prob[:], parent_probs[b][:], MULT)
-            nc.sync.dma_start(out[b * P : (b + 1) * P, :], joint[:])
+        def joint(b):
+            joint_prob = work.tile([P, CHILDREN], F32, name="joint_prob")
+            nc.vector.tensor_tensor(joint_prob[:], child_probs[b][:], parent_probs[b][:], MULT)
+            nc.sync.dma_start(out[b * P : (b + 1) * P, :], joint_prob[:])
+
+        for b in range(EARLY):
+            parent(b)
+        for b in range(EARLY):
+            child(b)
+            joint(b)
+        for b in range(EARLY, BLOCKS):
+            child(b)
+        for b in range(EARLY, BLOCKS):
+            parent(b)
+            joint(b)

@@ -10,8 +10,6 @@ PATIENTS = 512
 CHILDREN = 512
 BLOCKS = PATIENTS // P
 PIECE = PARENTS
-PIECES = CHILDREN // PIECE
-PIECE_COLS = PIECE // 16
 TOP_8, TOP_16, ALL_24 = -(1 << 16), -(1 << 8), -1
 KEEP = (TOP_8, TOP_16, ALL_24)
 DROP = (0, TOP_8, TOP_16)
@@ -96,32 +94,40 @@ def tile_hierarchicaldecoder_kernel(tc, w_parent, patients, w_child, b_child, of
             nc.scalar.activation(child_prob[:], child_bank[:], SIGMOID)
             child_probs[b] = child_prob
 
-        def parent(b):
-            parent_bank = psum.tile([P, CHILDREN], F32, name="parent_bank", bufs=EARLY)
-            for piece in range(PIECES):
-                nc.tensor.matmul(
-                    parent_bank[:, piece * PIECE : (piece + 1) * PIECE],
-                    patient_cols[:, b * P : (b + 1) * P],
-                    parent_table[:].indirect(offsets[:, piece * PIECE_COLS : (piece + 1) * PIECE_COLS]),
-                    start=True,
-                    stop=True,
-                )
+        def parent(b, banks=1, passes=1):
             parent_prob = work.tile([P, CHILDREN], F32, name="parent_prob")
-            nc.scalar.activation(parent_prob[:], parent_bank[:], SIGMOID)
+            columns = CHILDREN // banks
+            step = columns // passes
+            for first in range(0, CHILDREN, columns):
+                parent_bank = psum.tile([P, columns], F32, name="parent_bank", tag="first_bank" if b + first == 0 else "", bufs=1 if b + first == 0 else EARLY)
+                for j in range(first, first + columns, PIECE):
+                    nc.tensor.matmul(
+                        parent_bank[:, j - first : j - first + PIECE],
+                        patient_cols[:, b * P : (b + 1) * P],
+                        parent_table[:].indirect(offsets[:, j // 16 : (j + PIECE) // 16]),
+                        start=True,
+                        stop=True,
+                    )
+                for j in range(0, columns, step):
+                    nc.scalar.activation(parent_prob[:, first + j : first + j + step], parent_bank[:, j : j + step], SIGMOID)
             parent_probs[b] = parent_prob
 
-        def joint(b):
+        def joint(b, passes=1):
             joint_prob = work.tile([P, CHILDREN], F32, name="joint_prob")
-            nc.vector.tensor_tensor(joint_prob[:], child_probs[b][:], parent_probs[b][:], MULT)
-            nc.sync.dma_start(out[b * P : (b + 1) * P, :], joint_prob[:])
+            step = CHILDREN // passes
+            for j in range(0, CHILDREN, step):
+                cols = slice(j, j + step)
+                nc.vector.tensor_tensor(joint_prob[:, cols], child_probs[b][:, cols], parent_probs[b][:, cols], MULT)
+                nc.sync.dma_start(out[b * P : (b + 1) * P, cols], joint_prob[:, cols])
 
-        for b in range(EARLY):
-            parent(b)
+        parent(0, banks=2)
+        parent(1)
         for b in range(EARLY):
             child(b)
             joint(b)
         for b in range(EARLY, BLOCKS):
             child(b)
-        for b in range(EARLY, BLOCKS):
-            parent(b)
-            joint(b)
+        parent(2)
+        joint(2)
+        parent(3, passes=2)
+        joint(3, passes=2)

@@ -17,7 +17,7 @@ TERMS = len(KEEP)
 HALVES = 2
 HALF = CHILDREN // HALVES
 BIAS_ROWS = HALVES * TERMS
-EARLY = BLOCKS // 2
+LAST = BLOCKS - 1
 CHILD_PIECE = 128
 WARMUPS = 3
 
@@ -99,7 +99,7 @@ def tile_hierarchicaldecoder_kernel(tc, w_parent, patients, w_child, b_child, of
             columns = CHILDREN // banks
             step = columns // passes
             for first in range(0, CHILDREN, columns):
-                parent_bank = psum.tile([P, columns], F32, name="parent_bank", tag="first_bank" if b + first == 0 else "", bufs=1 if b + first == 0 else EARLY)
+                parent_bank = psum.tile([P, columns], F32, name="parent_bank", tag="first_bank" if b + first == 0 else "", bufs=1 if b + first == 0 else LAST)
                 for j in range(first, first + columns, PIECE):
                     nc.tensor.matmul(
                         parent_bank[:, j - first : j - first + PIECE],
@@ -121,13 +121,11 @@ def tile_hierarchicaldecoder_kernel(tc, w_parent, patients, w_child, b_child, of
                 nc.sync.dma_start(out[b * P : (b + 1) * P, cols], joint_prob[:, cols])
 
         parent(0, banks=2)
-        parent(1)
-        for b in range(EARLY):
+        for b in range(1, LAST):
+            parent(b)
+        for b in range(LAST):
             child(b)
             joint(b)
-        for b in range(EARLY, BLOCKS):
-            child(b)
-        parent(2)
-        joint(2)
-        parent(3, passes=2)
-        joint(3, passes=2)
+        child(LAST)
+        parent(LAST, passes=2)
+        joint(LAST, passes=2)

@@ -19,7 +19,7 @@ HALF = CHILDREN // HALVES
 BIAS_ROWS = HALVES * TERMS
 LAST = BLOCKS - 1
 CHILD_PIECE = 128
-WARMUPS = 3
+WARMUPS = 2
 
 FLOPS = 2 * P * PATIENTS * CHILDREN * 2
 
@@ -33,7 +33,7 @@ def tile_hierarchicaldecoder_kernel(tc, w_parent, patients, w_child, b_child, of
     ):
         zeros = held.tile([P, CHILDREN], BF16, name="zeros")
         nc.vector.memset(zeros[:], 0.0)
-        warm_bank = psum.tile([P, CHILDREN], F32, name="warm_bank", tag="child_bank")
+        warm_bank = psum.tile([P, CHILDREN], F32, name="warm_bank", tag="late_bank")
         for warmup in range(WARMUPS):
             nc.tensor.matmul(warm_bank[:], zeros[:, :P], zeros[:], start=True, stop=True)
 
@@ -42,11 +42,13 @@ def tile_hierarchicaldecoder_kernel(tc, w_parent, patients, w_child, b_child, of
         for term in range(TERMS):
             nc.scalar.dma_start(bias_copies[term::TERMS, :], bias_halves)
         patient_cols = held.tile([P, PATIENTS], BF16, name="patient_cols")
-        nc.sync.dma_start(patient_cols[:], patients)
+        first_patients, other_patients = slice(0, PATIENTS // 2), slice(PATIENTS // 2, PATIENTS)
+        nc.sync.dma_start(patient_cols[:, first_patients], patients[:, first_patients])
         offsets = held.tile([P, CHILDREN // 16], U16, name="offsets")
         nc.sync.dma_start(offsets[:], offs)
         parent_table = held.tile([P, PARENTS], BF16, name="parent_table")
         nc.sync.dma_start(parent_table[:], w_parent)
+        nc.sync.dma_start(patient_cols[:, other_patients], patients[:, other_patients])
         child_weights = held.tile([P, CHILDREN], BF16, name="child_weights")
         nc.sync.dma_start(child_weights[:], w_child)
 
@@ -73,7 +75,7 @@ def tile_hierarchicaldecoder_kernel(tc, w_parent, patients, w_child, b_child, of
         child_probs, parent_probs = {}, {}
 
         def child(b):
-            child_bank = psum.tile([P, CHILDREN], F32, name="child_bank")
+            child_bank = psum.tile([P, CHILDREN], F32, name="child_bank", tag="late_bank")
             for half in range(HALVES):
                 nc.tensor.matmul(
                     child_bank[:, half * HALF : (half + 1) * HALF],
@@ -94,12 +96,11 @@ def tile_hierarchicaldecoder_kernel(tc, w_parent, patients, w_child, b_child, of
             nc.scalar.activation(child_prob[:], child_bank[:], SIGMOID)
             child_probs[b] = child_prob
 
-        def parent(b, banks=1, passes=1):
+        def parent(b, tag, banks=1):
             parent_prob = work.tile([P, CHILDREN], F32, name="parent_prob")
             columns = CHILDREN // banks
-            step = columns // passes
             for first in range(0, CHILDREN, columns):
-                parent_bank = psum.tile([P, columns], F32, name="parent_bank", tag="first_bank" if b + first == 0 else "", bufs=1 if b + first == 0 else LAST)
+                parent_bank = psum.tile([P, columns], F32, name="parent_bank", tag=tag)
                 for j in range(first, first + columns, PIECE):
                     nc.tensor.matmul(
                         parent_bank[:, j - first : j - first + PIECE],
@@ -108,8 +109,7 @@ def tile_hierarchicaldecoder_kernel(tc, w_parent, patients, w_child, b_child, of
                         start=True,
                         stop=True,
                     )
-                for j in range(0, columns, step):
-                    nc.scalar.activation(parent_prob[:, first + j : first + j + step], parent_bank[:, j : j + step], SIGMOID)
+                nc.scalar.activation(parent_prob[:, first : first + columns], parent_bank[:], SIGMOID)
             parent_probs[b] = parent_prob
 
         def joint(b, passes=1):
@@ -120,12 +120,12 @@ def tile_hierarchicaldecoder_kernel(tc, w_parent, patients, w_child, b_child, of
                 nc.vector.tensor_tensor(joint_prob[:, cols], child_probs[b][:, cols], parent_probs[b][:, cols], MULT)
                 nc.sync.dma_start(out[b * P : (b + 1) * P, cols], joint_prob[:, cols])
 
-        parent(0, banks=2)
+        parent(0, "early_bank", banks=2)
         for b in range(1, LAST):
-            parent(b)
+            parent(b, "early_bank")
         for b in range(LAST):
             child(b)
             joint(b)
         child(LAST)
-        parent(LAST, passes=2)
+        parent(LAST, "late_bank", banks=2)
         joint(LAST, passes=2)

@@ -37,20 +37,20 @@ def tile_hierarchicaldecoder_kernel(tc, w_parent, patients, w_child, b_child, of
         for warmup in range(WARMUPS):
             nc.tensor.matmul(warm_bank[:], zeros[:, :P], zeros[:], start=True, stop=True)
 
-        bias_copies = held.tile([BIAS_ROWS, HALF], F32, name="bias_copies")
-        bias_halves = b_child.rearrange("o (h n) -> (o h) n", h=HALVES)
-        for term in range(TERMS):
-            nc.scalar.dma_start(bias_copies[term::TERMS, :], bias_halves)
-        patient_cols = held.tile([P, PATIENTS], BF16, name="patient_cols")
-        first_patients, other_patients = slice(0, PATIENTS // 2), slice(PATIENTS // 2, PATIENTS)
-        nc.sync.dma_start(patient_cols[:, first_patients], patients[:, first_patients])
         offsets = held.tile([P, CHILDREN // 16], U16, name="offsets")
         nc.sync.dma_start(offsets[:], offs)
         parent_table = held.tile([P, PARENTS], BF16, name="parent_table")
-        nc.sync.dma_start(parent_table[:], w_parent)
-        nc.sync.dma_start(patient_cols[:, other_patients], patients[:, other_patients])
+        nc.scalar.dma_start(parent_table[:], w_parent)
+        patient_cols = held.tile([P, PATIENTS], BF16, name="patient_cols")
+        first_patients, other_patients = slice(0, PATIENTS // 2), slice(PATIENTS // 2, PATIENTS)
+        nc.sync.dma_start(patient_cols[:, first_patients], patients[:, first_patients])
+        bias_copies = held.tile([BIAS_ROWS, HALF], F32, name="bias_copies")
+        bias_halves = b_child.rearrange("o (h n) -> (o h) n", h=HALVES)
+        for term in range(TERMS):
+            nc.sync.dma_start(bias_copies[term::TERMS, :], bias_halves)
+        nc.scalar.dma_start(patient_cols[:, other_patients], patients[:, other_patients])
         child_weights = held.tile([P, CHILDREN], BF16, name="child_weights")
-        nc.sync.dma_start(child_weights[:], w_child)
+        nc.scalar.dma_start(child_weights[:], w_child)
 
         keep_mask = held.tile([BIAS_ROWS, 1], I32, name="keep_mask")
         drop_mask = held.tile([BIAS_ROWS, 1], I32, name="drop_mask")

@@ -19,7 +19,7 @@ HALF = CHILDREN // HALVES
 BIAS_ROWS = HALVES * TERMS
 LAST = BLOCKS - 1
 CHILD_PIECE = 128
-WARMUPS = 2
+WARMUPS = 3
 
 FLOPS = 2 * P * PATIENTS * CHILDREN * 2
 
@@ -31,11 +31,12 @@ def tile_hierarchicaldecoder_kernel(tc, w_parent, patients, w_child, b_child, of
         tc.tile_pool(name="work", bufs=BLOCKS) as work,
         tc.psum_pool(name="psum", bufs=BLOCKS) as psum,
     ):
-        zeros = held.tile([P, CHILDREN], BF16, name="zeros")
+        zeros = held.tile([P, P], BF16, name="zeros")
         nc.vector.memset(zeros[:], 0.0)
+        many_zeros = zeros[:].unsqueeze(1).to_broadcast([P, CHILDREN // P, P])
         warm_bank = psum.tile([P, CHILDREN], F32, name="warm_bank", tag="late_bank")
         for warmup in range(WARMUPS):
-            nc.tensor.matmul(warm_bank[:], zeros[:, :P], zeros[:], start=True, stop=True)
+            nc.tensor.matmul(warm_bank[:], zeros[:], many_zeros, start=True, stop=True)
 
         offsets = held.tile([P, CHILDREN // 16], U16, name="offsets")
         nc.sync.dma_start(offsets[:], offs)

import concourse.mybir as mybir

BF16, F32, U16, I32 = mybir.dt.bfloat16, mybir.dt.float32, mybir.dt.uint16, mybir.dt.int32
SIGMOID = mybir.ActivationFunctionType.Sigmoid
MULT, SUBTRACT, AND = mybir.AluOpType.mult, mybir.AluOpType.subtract, mybir.AluOpType.bitwise_and

P = 128
PARENTS = 256
PATIENTS = 512
CHILDREN = 512
BLOCKS = PATIENTS // P
PIECE = PARENTS
TOP_8, TOP_16, ALL_24 = -(1 << 16), -(1 << 8), -1
KEEP = (TOP_8, TOP_16, ALL_24)
DROP = (0, TOP_8, TOP_16)
TERMS = len(KEEP)
HALVES = 2
HALF = CHILDREN // HALVES
BIAS_ROWS = HALVES * TERMS
LAST = BLOCKS - 1
CHILD_PIECE = 128
WARMUPS = 3

FLOPS = 2 * P * PATIENTS * CHILDREN * 2


def tile_hierarchicaldecoder_kernel(tc, w_parent, patients, w_child, b_child, offs, out):
    nc = tc.nc
    with (
        tc.tile_pool(name="held", bufs=1) as held,
        tc.tile_pool(name="work", bufs=BLOCKS) as work,
        tc.psum_pool(name="psum", bufs=BLOCKS) as psum,
    ):
        zeros = held.tile([P, P], BF16, name="zeros")
        nc.vector.memset(zeros[:], 0.0)
        many_zeros = zeros[:].unsqueeze(1).to_broadcast([P, CHILDREN // P, P])
        warm_bank = psum.tile([P, CHILDREN], F32, name="warm_bank", tag="late_bank")
        for warmup in range(WARMUPS):
            nc.tensor.matmul(warm_bank[:], zeros[:], many_zeros, start=True, stop=True)

        offsets = held.tile([P, CHILDREN // 16], U16, name="offsets")
        nc.sync.dma_start(offsets[:], offs)
        parent_table = held.tile([P, PARENTS], BF16, name="parent_table")
        nc.scalar.dma_start(parent_table[:], w_parent)
        patient_cols = held.tile([P, PATIENTS], BF16, name="patient_cols")
        first_patients, other_patients = slice(0, PATIENTS // 2), slice(PATIENTS // 2, PATIENTS)
        nc.sync.dma_start(patient_cols[:, first_patients], patients[:, first_patients])
        bias_copies = held.tile([BIAS_ROWS, HALF], F32, name="bias_copies")
        bias_halves = b_child.rearrange("o (h n) -> (o h) n", h=HALVES)
        for term in range(TERMS):
            nc.sync.dma_start(bias_copies[term::TERMS, :], bias_halves)
        nc.scalar.dma_start(patient_cols[:, other_patients], patients[:, other_patients])
        child_weights = held.tile([P, CHILDREN], BF16, name="child_weights")
        nc.scalar.dma_start(child_weights[:], w_child)

        keep_mask = held.tile([BIAS_ROWS, 1], I32, name="keep_mask")
        drop_mask = held.tile([BIAS_ROWS, 1], I32, name="drop_mask")
        for row in reversed(range(BIAS_ROWS)):
            nc.vector.memset(keep_mask[: row + 1, :], KEEP[row % TERMS])
            nc.vector.memset(drop_mask[: row + 1, :], DROP[row % TERMS])
        selectors = held.tile([P, HALVES * P], BF16, name="selectors")
        nc.vector.memset(selectors[:], 0.0)
        for half in range(HALVES):
            selector = selectors[:, half * P : (half + 1) * P]
            nc.vector.memset(selector[: (half + 1) * TERMS, :], 1.0)
            if half > 0:
                nc.vector.memset(selector[: half * TERMS, :], 0.0)
        bias_terms = held.tile([P, HALF], BF16, name="bias_terms")
        nc.vector.memset(bias_terms[:], 0.0)
        kept = held.tile([BIAS_ROWS, HALF], I32, name="kept")
        nc.vector.tensor_scalar(kept[:], bias_copies[:].bitcast(I32), keep_mask[:, 0:1], None, AND)
        dropped = held.tile([BIAS_ROWS, HALF], I32, name="dropped")
        nc.vector.tensor_scalar(dropped[:], bias_copies[:].bitcast(I32), drop_mask[:, 0:1], None, AND)
        nc.vector.tensor_tensor(bias_terms[:BIAS_ROWS, :], kept[:].bitcast(F32), dropped[:].bitcast(F32), SUBTRACT)

        child_probs, parent_probs = {}, {}

        def child(b):
            child_bank = psum.tile([P, CHILDREN], F32, name="child_bank", tag="late_bank")
            for half in range(HALVES):
                nc.tensor.matmul(
                    child_bank[:, half * HALF : (half + 1) * HALF],
                    selectors[:, half * P : (half + 1) * P],
                    bias_terms[:],
                    start=half == 0,
                    stop=False,
                )
            for first in range(0, CHILDREN, CHILD_PIECE):
                nc.tensor.matmul(
                    child_bank[:, first : first + CHILD_PIECE],
                    patient_cols[:, b * P : (b + 1) * P],
                    child_weights[:, first : first + CHILD_PIECE],
                    start=False,
                    stop=first + CHILD_PIECE == CHILDREN,
                )
            child_prob = work.tile([P, CHILDREN], F32, name="child_prob")
            nc.scalar.activation(child_prob[:], child_bank[:], SIGMOID)
            child_probs[b] = child_prob

        def parent(b, tag, banks=1):
            parent_prob = work.tile([P, CHILDREN], F32, name="parent_prob")
            columns = CHILDREN // banks
            for first in range(0, CHILDREN, columns):
                parent_bank = psum.tile([P, columns], F32, name="parent_bank", tag=tag)
                for j in range(first, first + columns, PIECE):
                    nc.tensor.matmul(
                        parent_bank[:, j - first : j - first + PIECE],
                        patient_cols[:, b * P : (b + 1) * P],
                        parent_table[:].indirect(offsets[:, j // 16 : (j + PIECE) // 16]),
                        start=True,
                        stop=True,
                    )
                nc.scalar.activation(parent_prob[:, first : first + columns], parent_bank[:], SIGMOID)
            parent_probs[b] = parent_prob

        def joint(b, passes=1):
            joint_prob = work.tile([P, CHILDREN], F32, name="joint_prob")
            step = CHILDREN // passes
            for j in range(0, CHILDREN, step):
                cols = slice(j, j + step)
                nc.vector.tensor_tensor(joint_prob[:, cols], child_probs[b][:, cols], parent_probs[b][:, cols], MULT)
                nc.sync.dma_start(out[b * P : (b + 1) * P, cols], joint_prob[:, cols])

        parent(0, "early_bank", banks=2)
        for b in range(1, LAST):
            parent(b, "early_bank")
        for b in range(LAST):
            child(b)
            joint(b)
        child(LAST)
        parent(LAST, "late_bank", banks=2)
        joint(LAST, passes=2)
